import numpy as np
import ml_dtypes


def mxq(x, axis, fmt="e4m3"):
    dtype, down = {"e4m3": (ml_dtypes.float8_e4m3fn, 7), "e5m2": (ml_dtypes.float8_e5m2, 14)}[fmt]
    v = np.moveaxis(np.asarray(x, np.float32).astype(ml_dtypes.bfloat16).astype(np.float64), axis, -1)
    blocks = v.reshape(v.shape[:-1] + (-1, 32))
    amax = np.abs(blocks).max(-1, keepdims=True)
    byte = np.maximum(np.where(amax > 0, np.frexp(amax)[1] - 1 + 127, 0) - down, 1)
    scale = np.exp2(byte - 127.0)
    codes = (blocks / scale).astype(np.float32).astype(dtype).astype(np.float64)
    return np.moveaxis((codes * scale).reshape(v.shape), -1, axis)


WIDE = False


def mx_kscale(k):
    if not WIDE:
        return np.ones(k)
    levels = np.array([10, -10, 5, -5, 0])
    if k % 512:
        return np.exp2(np.random.permutation(np.resize(levels, k // 32))).repeat(32)
    a = np.empty((k // 512, 16))
    for p in range(k // 512):
        a[p, :8] = np.random.permutation(np.resize(levels, 8))
        for g in range(8):
            far = levels[np.abs(levels - a[p, g]) >= 10]
            a[p, g + 8] = far[np.random.randint(len(far))]
    return np.exp2(a.ravel()).repeat(32)


BF16 = ml_dtypes.bfloat16


def bf(x):
    return np.asarray(x, np.float32).astype(BF16)


def f64(x):
    return np.asarray(x).astype(np.float64)


E2M1 = np.array([0.0, 0.5, 1.0, 1.5, 2.0, 3.0, 4.0, 6.0, -0.0, -0.5, -1.0, -1.5, -2.0, -3.0, -4.0, -6.0])


def pack_weight(w, fmt):
    k, n = w.shape
    w = f64(bf(w)).reshape(k // 32, 32, n)
    amax = np.abs(w).max(1)
    if fmt == "e4m3":
        byte = np.frexp(amax)[1] - 1 + 127 - 7
    else:
        mant, ex = np.frexp(amax / 6.0)
        byte = np.where(mant > 0.5, ex, ex - 1) + 127
    byte = np.clip(np.where(amax > 0, byte, 1), 1, 254)
    scaled = (w * np.exp2(127.0 - byte)[:, None, :]).reshape(k, n).astype(np.float32)
    by_word = np.ascontiguousarray(scaled.reshape(k // 512, 128, 4, n).transpose(0, 1, 3, 2))
    if fmt == "e4m3":
        words = by_word.astype(ml_dtypes.float8_e4m3fn).view(np.uint8)
    else:
        c = by_word.astype(ml_dtypes.float4_e2m1fn).view(np.uint8) & 0xF
        words = c[..., 0::2] | (c[..., 1::2] << 4)
    return np.ascontiguousarray(words), np.ascontiguousarray(byte.astype(np.uint8).reshape(k // 512, 16, n))


def unpack_weight(words, scales, fmt):
    g, p, n, _ = words.shape
    if fmt == "e4m3":
        vals = np.ascontiguousarray(words).view(ml_dtypes.float8_e4m3fn).astype(np.float64)
    else:
        nib = np.empty((g, p, n, 4), np.uint8)
        nib[..., 0::2] = words & 0xF
        nib[..., 1::2] = words >> 4
        vals = E2M1[nib]
    vals = vals * np.repeat(np.exp2(scales.astype(np.float64) - 127.0), 8, axis=1)[..., None]
    return vals.transpose(0, 1, 3, 2).reshape(g * 512, n)
def pack4(w):
    words, scales = pack_weight(w, "e2m1")
    return words.reshape(words.shape[0], 128, -1), scales


def unpack4(words, scales):
    return unpack_weight(words.reshape(words.shape[0], 128, -1, 2), scales, "e2m1")


B, S, E, H, DH, L = 2, 512, 2048, 16, 128, 512
NOPE = DH // 4
ROPE_D = DH - NOPE
THETA = 10000.0


def rope_tables(seq_len):
    freqs = 1.0 / THETA ** (np.arange(0, ROPE_D, 2) / ROPE_D)
    emb = np.arange(seq_len)[:, None] * freqs[None, :]
    return np.cos(emb), np.sin(emb)


def apply_rope(x, cos, sin):
    xe, xo = x[..., ::2], x[..., 1::2]
    return np.concatenate([xe * cos - xo * sin, xo * cos + xe * sin], axis=-1)


def draw0():
    s, t = mx_kscale(E), mx_kscale(L)
    x = bf(np.random.standard_normal((B, S, E)) * s)
    down_words, down_scales = pack4(np.random.standard_normal((E, L)) / np.sqrt(E) / s[:, None] * t)
    k_words, k_scales = pack4(np.random.standard_normal((L, H * DH)) / np.sqrt(L) / t[:, None])
    v_words, v_scales = pack4(np.random.standard_normal((L, H * DH)) / np.sqrt(L) / t[:, None])
    return {"x": x,
            "Wkv_down_words": down_words, "Wkv_down_scales": down_scales,
            "Wk_up_words": k_words, "Wk_up_scales": k_scales,
            "Wv_up_words": v_words, "Wv_up_scales": v_scales}


def core(x, Wkv_down_words, Wkv_down_scales, Wk_up_words, Wk_up_scales, Wv_up_words, Wv_up_scales):
    c_kv = mxq(f64(x), 2, "e4m3") @ unpack4(Wkv_down_words, Wkv_down_scales)
    cq = mxq(c_kv, 2, "e4m3")
    k = (cq @ unpack4(Wk_up_words, Wk_up_scales)).reshape(B, S, H, DH).transpose(0, 2, 1, 3)
    v = (cq @ unpack4(Wv_up_words, Wv_up_scales)).reshape(B, S, H, DH).transpose(0, 2, 1, 3)
    k_nope, k_rope = k[..., :NOPE], k[..., NOPE:]
    cos, sin = rope_tables(S)
    k_rope = apply_rope(k_rope, cos, sin)
    kf = np.concatenate([k_nope, k_rope], axis=-1)
    return kf, v


def e4m3fn_bytes(y):
    return np.clip(np.asarray(y, np.float64), -448.0, 448.0).astype(np.float32).astype(ml_dtypes.float8_e4m3fn).view(np.uint8)


def e4m3fn_values(b):
    return np.asarray(b, np.uint8).view(ml_dtypes.float8_e4m3fn).astype(np.float64)


def setup_inputs():
    d = draw0()
    x0 = np.asarray(d['x']).astype(np.float64)
    s = (np.max(np.abs(x0), axis=(0, 1), keepdims=True) / 448.0).astype(np.float32)
    out = {}
    for k, v in d.items():
        if k == 'x':
            out['x_bytes'] = e4m3fn_bytes(x0 / s.astype(np.float64))
            out['x_scale'] = s
        else:
            out[k] = v
    return out


def reference(x_bytes, x_scale, Wkv_down_words, Wkv_down_scales, Wk_up_words, Wk_up_scales, Wv_up_words, Wv_up_scales):
    return core(e4m3fn_values(x_bytes) * x_scale.astype(np.float64), Wkv_down_words, Wkv_down_scales, Wk_up_words, Wk_up_scales, Wv_up_words, Wv_up_scales)

@@ -1,0 +1,270 @@
+import math
+from contextlib import ExitStack
+
+import concourse.mybir as mybir
+from concourse.masks import make_identity
+
+F32 = mybir.dt.float32
+BF16 = mybir.dt.bfloat16
+I32 = mybir.dt.int32
+U32 = mybir.dt.uint32
+U8 = mybir.dt.uint8
+FP8 = mybir.dt.float8_e4m3fn
+FP8X4 = mybir.dt.float8_e4m3fn_x4
+FP4X4 = mybir.dt.float4_e2m1fn_x4
+ALU = mybir.AluOpType
+ACT = mybir.ActivationFunctionType
+
+B, S, E, H, DH, L = 2, 512, 2048, 16, 128, 512
+NOPE = DH // 4
+ROPE = DH - NOPE
+HALF = ROPE // 2
+THETA = 10000.0
+P = 128
+T = 2
+Q = S // (T * P)
+NU = B * Q
+G = E // 512
+HB = 512 // DH
+NG = H // HB
+
+FLOPS = 2 * B * S * E * L + 2 * 2 * B * S * L * H * DH
+
+
+def tile_mla_pa_w4_kernel(tc, x_bytes, x_scale, wd_words, wd_scales, wk_words, wk_scales,
+                                      wv_words, wv_scales, out_k, out_v):
+    nc = tc.nc
+    with ExitStack() as ctx:
+        keep = ctx.enter_context(tc.tile_pool(name="keep", bufs=1))
+        xbp = ctx.enter_context(tc.tile_pool(name="xbp", bufs=8))
+        work = ctx.enter_context(tc.tile_pool(name="work", bufs=3))
+        outp = ctx.enter_context(tc.tile_pool(name="outp", bufs=8))
+        ps_x = ctx.enter_context(tc.psum_pool(name="ps_x", bufs=2))
+        ps_c = ctx.enter_context(tc.psum_pool(name="ps_c", bufs=2))
+        ps_u = ctx.enter_context(tc.psum_pool(name="ps_u", bufs=4))
+
+        ident = keep.tile([P, P], F32, name="ident")
+        wd = keep.tile([P, G, 2 * L], U8, name="wd", align_bytes=64)
+        wds = keep.tile([P, G, L], U8, name="wds", align_bytes=64)
+        wk = keep.tile([P, 2 * H * DH], U8, name="wk", align_bytes=64)
+        wks = keep.tile([P, H * DH], U8, name="wks", align_bytes=64)
+        wv = keep.tile([P, 2 * H * DH], U8, name="wv", align_bytes=64)
+        wvs = keep.tile([P, H * DH], U8, name="wvs", align_bytes=64)
+        xsc = keep.tile([P, E], F32, name="xsc")
+        xb = [xbp.tile([P, E], U8, name="xb", align_bytes=64) for i in range(NU * T)]
+
+        pos = keep.tile([P, Q, T], F32, name="pos")
+        nc.gpsimd.iota(pos[:], pattern=[[T * P, Q], [1, T]], base=0, channel_multiplier=T, allow_small_or_imprecise_dtypes=True)
+        nc.gpsimd.memset(wds[:].rearrange("p g n -> p (g n)").bitcast(I32), 0)
+        make_identity(nc, ident[:])
+        nc.gpsimd.memset(wvs[:].bitcast(I32), 0)
+        nc.gpsimd.memset(wks[:].bitcast(I32), 0)
+
+        def load_x(i):
+            u, t = divmod(i, T)
+            b, q = divmod(u, Q)
+            nc.sync.dma_start(out=xb[i][:], in_=x_bytes[b].rearrange("(q p t) k -> q t p k", q=Q, t=T)[q, t])
+
+        def load_scale(h):
+            row = x_scale.rearrange("a b k -> (a b k)")
+            cols = slice(h * (E // 2), (h + 1) * (E // 2))
+            nc.sync.dma_start(out=xsc[:, cols], in_=row[cols].partition_broadcast(P))
+
+        load_x(0)
+        load_scale(0)
+        load_scale(1)
+        load_x(1)
+        nc.sync.dma_start(out=wd[:], in_=wd_words.rearrange("g p n -> p g n"))
+        for q in range(4):
+            nc.sync.dma_start(out=wds[32 * q:32 * q + 4, :, :].bitcast(I32),
+                              in_=wd_scales[:, 4 * q:4 * q + 4, :].rearrange("g q n -> q g n").bitcast(I32))
+        load_x(2)
+        load_x(3)
+        nc.sync.dma_start(out=wv[:], in_=wv_words[0])
+        for q in range(4):
+            nc.sync.dma_start(out=wvs[32 * q:32 * q + 4, :].bitcast(I32),
+                              in_=wv_scales[0, 4 * q:4 * q + 4, :].bitcast(I32))
+        nc.sync.dma_start(out=wk[:], in_=wk_words[0])
+        for q in range(4):
+            nc.sync.dma_start(out=wks[32 * q:32 * q + 4, :].bitcast(I32),
+                              in_=wk_scales[0, 4 * q:4 * q + 4, :].bitcast(I32))
+        for i in range(4, NU * T):
+            load_x(i)
+
+        turn = keep.tile([P, HALF], F32, name="turn")
+        ph = keep.tile([P, 2, Q * T, HALF], F32, name="ph")
+        phi = keep.tile([P, 2, Q * T, HALF], I32, name="phi")
+        over = keep.tile([P, 2, Q * T, HALF], F32, name="over")
+        cos = keep.tile([P, Q * T, ROPE], F32, name="cos")
+        sin = keep.tile([P, Q * T, ROPE], F32, name="sin")
+        warm = keep.tile([P, 1], F32, name="warm")
+        nc.vector.memset(warm[:], 0.0)
+        nc.scalar.activation(out=warm[:], in_=warm[:], func=ACT.Sin)
+        nc.vector.memset(turn[:, 0:1], 1.0)
+        n = 1
+        while n < HALF:
+            m = min(n, HALF - n)
+            nc.vector.tensor_scalar(out=turn[:, n:n + m], in0=turn[:, 0:m], scalar1=THETA ** (-2.0 * n / ROPE),
+                                    scalar2=None, op0=ALU.mult)
+            n += m
+        nc.vector.tensor_scalar(out=turn[:], in0=turn[:], scalar1=1.0 / (2.0 * math.pi), scalar2=None, op0=ALU.mult)
+        nc.vector.tensor_tensor(out=ph[:, 1, :, :], in0=turn[:].unsqueeze(1).to_broadcast([P, Q * T, HALF]),
+                                in1=pos[:].rearrange("p q t -> p (q t)").unsqueeze(2).to_broadcast([P, Q * T, HALF]),
+                                op=ALU.mult)
+        nc.vector.tensor_scalar(out=ph[:, 0, :, :], in0=ph[:, 1, :, :], scalar1=0.25, scalar2=None, op0=ALU.add)
+        nc.vector.tensor_copy(out=phi[:], in_=ph[:])
+        nc.vector.tensor_tensor(out=ph[:], in0=ph[:], in1=phi[:], op=ALU.subtract)
+        nc.vector.tensor_scalar(out=over[:], in0=ph[:], scalar1=0.5, scalar2=None, op0=ALU.is_gt)
+        nc.vector.tensor_tensor(out=ph[:], in0=ph[:], in1=over[:], op=ALU.subtract)
+        lo, hi = slice(0, HALF), slice(HALF, ROPE)
+        nc.scalar.activation(out=cos[:, :, lo], in_=ph[:, 0, :, :], func=ACT.Sin, scale=2.0 * math.pi)
+        nc.scalar.activation(out=cos[:, :, hi], in_=ph[:, 0, :, :], func=ACT.Sin, scale=2.0 * math.pi)
+        nc.scalar.activation(out=sin[:, :, lo], in_=ph[:, 1, :, :], func=ACT.Sin, scale=-2.0 * math.pi)
+        nc.scalar.activation(out=sin[:, :, hi], in_=ph[:, 1, :, :], func=ACT.Sin, scale=2.0 * math.pi)
+
+        N = NU * T
+        xs, xt, xq, xqs, cs, ct, cq, cqs = ({}, {}, {}, {}, {}, {}, {}, {})
+        bank, cbank = ({}, {})
+        for i in range(N):
+            cq[i] = keep.tile([P, P], U32, name="cq%d" % i, align_bytes=64)
+            cqs[i] = keep.tile([P, P], U8, name="cqs%d" % i, align_bytes=64)
+
+        def product(i):
+            xs[i] = work.tile([P, E], BF16, name="xs", align_bytes=64)
+            parts = 2 if i == 0 else 1
+            for h in range(parts):
+                cols = slice(h * (E // parts), (h + 1) * (E // parts))
+                nc.vector.tensor_tensor(out=xs[i][:, cols], in0=xb[i][:, cols].bitcast(FP8), in1=xsc[:, cols], op=ALU.mult)
+
+        def turn_x(i):
+            words = xs[i][:].bitcast(F32)
+            xt[i] = work.tile([P, G * P * 4], BF16, name="xt", align_bytes=64)
+            for h in range(2):
+                bk = ps_x.tile([P, 2, 2, P], F32, name="xbank")
+                for gg in range(2):
+                    for u in range(2):
+                        g = 2 * h + gg
+                        nc.tensor.transpose(bk[:, gg, u, :], words[:, 256 * g + u:256 * (g + 1):2], ident[:])
+                bank[(i, h)] = bk
+
+        def copy_x(i):
+            dst = xt[i][:].bitcast(F32).rearrange("p (g r u) -> p g r u", g=G, u=2)
+            for h in range(2):
+                nc.scalar.copy(out=dst[:, 2 * h:2 * h + 2, :, :], in_=bank[(i, h)][:].rearrange("p g u r -> p g r u"))
+
+        def quant_x(i):
+            xq[i] = work.tile([P, G * P], U32, name="xq", align_bytes=64)
+            xqs[i] = work.tile([P, G * P], U8, name="xqs", align_bytes=64)
+            nc.vector.quantize_mx(out=xq[i][:].bitcast(FP8X4), scales=xqs[i][:], in_=xt[i][:])
+
+        def down(i):
+            acc = ps_c.tile([P, L], F32, name="cbank")
+            for g in range(G):
+                nc.tensor.matmul_mx(out=acc[:], lhsT=xq[i][:, g * P:(g + 1) * P].bitcast(FP8X4),
+                                    lhsT_scale=xqs[i][:, g * P:(g + 1) * P],
+                                    rhs=wd[:, g, :].bitcast(FP4X4), rhs_scale=wds[:, g, :],
+                                    start=(g == 0), stop=(g == G - 1))
+            cs[i] = work.tile([P, L], BF16, name="cs", align_bytes=64)
+            cbank[i] = acc
+
+        def copy_c(i):
+            nc.scalar.copy(out=cs[i][:], in_=cbank[i][:])
+
+        def turn_c(i):
+            words = cs[i][:].bitcast(F32)
+            bk = ps_c.tile([P, 2, P], F32, name="cbank")
+            for u in range(2):
+                nc.tensor.transpose(bk[:, u, :], words[:, u:256:2], ident[:])
+            cbank[i] = bk
+
+        def copy_ct(i):
+            ct[i] = work.tile([P, 4 * P], BF16, name="ct", align_bytes=64)
+            nc.scalar.copy(out=ct[i][:].bitcast(F32).rearrange("p (r u) -> p r u", u=2),
+                           in_=cbank[i][:].rearrange("p u r -> p r u"))
+
+        def quant_c(i):
+            nc.vector.quantize_mx(out=cq[i][:].bitcast(FP8X4), scales=cqs[i][:], in_=ct[i][:])
+
+        okt, ovt = ({}, {})
+
+        def up(i, w, ws, g):
+            bk = ps_u.tile([P, 512], F32, name="ubank")
+            nc.tensor.matmul_mx(out=bk[:], lhsT=cq[i][:].bitcast(FP8X4), lhsT_scale=cqs[i][:],
+                                rhs=w[:, 1024 * g:1024 * (g + 1)].bitcast(FP4X4), rhs_scale=ws[:, 512 * g:512 * (g + 1)],
+                                start=True, stop=True)
+            return bk
+
+        def store(out, tl, u, g, t0, t1):
+            b, q = divmod(u, Q)
+            nc.sync.dma_start(
+                out=out[b, g * HB:(g + 1) * HB].rearrange("h (q p t) d -> q p h t d", q=Q, t=T)[q, :, :, t0:t1, :]
+                .rearrange("p h t d -> p h (t d)"),
+                in_=tl[:, :, t0:t1, :].rearrange("p h t d -> p h (t d)"))
+
+        done = {}
+
+        def finish(kind, out, tiles, u, g, t):
+            key = (kind, u, g)
+            done[key] = done.get(key, 0) + 1
+            if done[key] == T:
+                store(out, tiles[(u, g)], u, g, 0, T)
+
+        def value(u, g, t):
+            bk = up(u * T + t, wv, wvs, g)
+            if (u, g) not in ovt:
+                ovt[(u, g)] = outp.tile([P, HB, T, DH], F32, name="ov")
+            nc.scalar.copy(out=ovt[(u, g)][:, :, t, :], in_=bk[:].rearrange("p (h d) -> p h d", h=HB))
+            finish("v", out_v, ovt, u, g, t)
+
+        def key(u, g, t):
+            bk = up(u * T + t, wk, wks, g)
+            if (u, g) not in okt:
+                okt[(u, g)] = outp.tile([P, HB, T, DH], F32, name="ok")
+            dst = okt[(u, g)][:, :, t, :]
+            src = bk[:].rearrange("p (h d) -> p h d", h=HB)
+            rot = src[:, :, NOPE:DH].rearrange("p h (j e) -> p h e j", e=2)
+            nc.scalar.copy(out=dst[:, :, 0:NOPE], in_=src[:, :, 0:NOPE])
+            w = (u % Q) * T + t
+            cosb = cos[:, w, :].rearrange("p (e j) -> p e j", e=2).unsqueeze(1).to_broadcast([P, HB, 2, HALF])
+            sinb = sin[:, w, :].rearrange("p (e j) -> p e j", e=2).unsqueeze(1).to_broadcast([P, HB, 2, HALF])
+            r1 = work.tile([P, HB, ROPE], F32, name="r1")
+            r2 = work.tile([P, HB, ROPE], F32, name="r2")
+            nc.vector.tensor_tensor(out=r1[:].rearrange("p h (e j) -> p h e j", e=2), in0=rot, in1=cosb, op=ALU.mult)
+            nc.vector.tensor_tensor(out=r2[:].rearrange("p h (e j) -> p h e j", e=2), in0=rot[:, :, ::-1, :], in1=sinb,
+                                    op=ALU.mult)
+            last = (u, g, t) == (NU - 1, NG - 1, T - 1)
+            adder = nc.vector if last else nc.gpsimd
+            adder.tensor_tensor(out=dst[:, :, NOPE:DH], in0=r1[:], in1=r2[:], op=ALU.add)
+            finish("k", out_k, okt, u, g, t)
+
+        order = [(0, 0), (1, 0), (0, 1), (1, 1), (2, 0), (3, 0), (2, 1), (3, 1)]
+        keys = [(u, g, t) for u in range(NU) for g, t in order]
+        vals = [(u, g, t) for u in range(NU) for g, t in order]
+        n_keys = [0, 0, 0, 2, 4, 4, 4, 4]
+        n_vals = [0, 0, 0, 2, 4, 4, 4, 4]
+        for s in range(N + 3):
+            if 0 <= s - 2 < N:
+                turn_c(s - 2)
+                copy_ct(s - 2)
+            if s < N:
+                product(s)
+                turn_x(s)
+                copy_x(s)
+            if 0 <= s - 1 < N:
+                quant_x(s - 1)
+                down(s - 1)
+                copy_c(s - 1)
+            nk = n_keys[s] if s < N else 2
+            nv = n_vals[s] if s < N else 2
+            for r in range(max(nk, nv)):
+                if r < nv:
+                    value(*vals.pop(0))
+                if r < nk:
+                    key(*keys.pop(0))
+            if 0 <= s - 2 < N:
+                quant_c(s - 2)
+        while keys or vals:
+            if vals:
+                value(*vals.pop(0))
+            if keys:
+                key(*keys.pop(0))

@@ -50,7 +50,7 @@ def tile_mla_pa_w4_kernel(tc, x_bytes, x_scale, wd_words, wd_scales, wk_words, w
         wks = keep.tile([P, H * DH], U8, name="wks", align_bytes=64)
         wv = keep.tile([P, 2 * H * DH], U8, name="wv", align_bytes=64)
         wvs = keep.tile([P, H * DH], U8, name="wvs", align_bytes=64)
-        xsc = keep.tile([P, E], F32, name="xsc")
+        xsc = keep.tile([P, G, 4], F32, name="xsc")
         xb = [xbp.tile([P, E], U8, name="xb", align_bytes=64) for i in range(NU * T)]
 
         pos = keep.tile([P, Q, T], F32, name="pos")
@@ -65,14 +65,8 @@ def tile_mla_pa_w4_kernel(tc, x_bytes, x_scale, wd_words, wd_scales, wk_words, w
             b, q = divmod(u, Q)
             nc.sync.dma_start(out=xb[i][:], in_=x_bytes[b].rearrange("(q p t) k -> q t p k", q=Q, t=T)[q, t])
 
-        def load_scale(h):
-            row = x_scale.rearrange("a b k -> (a b k)")
-            cols = slice(h * (E // 2), (h + 1) * (E // 2))
-            nc.sync.dma_start(out=xsc[:, cols], in_=row[cols].partition_broadcast(P))
-
         load_x(0)
-        load_scale(0)
-        load_scale(1)
+        nc.sync.dma_start(out=xsc[:], in_=x_scale.rearrange("a b (g p t) -> p (a b g) t", p=P, t=4))
         load_x(1)
         nc.sync.dma_start(out=wd[:], in_=wd_words.rearrange("g p n -> p g n"))
         for q in range(4):
@@ -129,28 +123,31 @@ def tile_mla_pa_w4_kernel(tc, x_bytes, x_scale, wd_words, wd_scales, wk_words, w
             cq[i] = keep.tile([P, P], U32, name="cq%d" % i, align_bytes=64)
             cqs[i] = keep.tile([P, P], U8, name="cqs%d" % i, align_bytes=64)
 
-        def product(i):
+        def widen(i):
             xs[i] = work.tile([P, E], BF16, name="xs", align_bytes=64)
-            parts = 2 if i == 0 else 1
-            for h in range(parts):
-                cols = slice(h * (E // parts), (h + 1) * (E // parts))
-                nc.vector.tensor_tensor(out=xs[i][:, cols], in0=xb[i][:, cols].bitcast(FP8), in1=xsc[:, cols], op=ALU.mult)
+            if i == 0:
+                nc.vector.tensor_copy(out=xs[i][:], in_=xb[i][:].bitcast(FP8))
+            else:
+                nc.scalar.copy(out=xs[i][:], in_=xb[i][:].bitcast(FP8))
 
         def turn_x(i):
             words = xs[i][:].bitcast(F32)
             xt[i] = work.tile([P, G * P * 4], BF16, name="xt", align_bytes=64)
             for h in range(2):
-                bk = ps_x.tile([P, 2, 2, P], F32, name="xbank")
+                bk = ps_x.tile([P, 2, P, 2], F32, name="xbank")
                 for gg in range(2):
                     for u in range(2):
                         g = 2 * h + gg
-                        nc.tensor.transpose(bk[:, gg, u, :], words[:, 256 * g + u:256 * (g + 1):2], ident[:])
+                        nc.tensor.transpose(bk[:, gg, :, u], words[:, 256 * g + u:256 * (g + 1):2], ident[:])
                 bank[(i, h)] = bk
 
-        def copy_x(i):
-            dst = xt[i][:].bitcast(F32).rearrange("p (g r u) -> p g r u", g=G, u=2)
+        def product(i):
+            dst = xt[i][:].rearrange("p (g r j) -> p g r j", g=G, j=4)
             for h in range(2):
-                nc.scalar.copy(out=dst[:, 2 * h:2 * h + 2, :, :], in_=bank[(i, h)][:].rearrange("p g u r -> p g r u"))
+                gs = slice(2 * h, 2 * h + 2)
+                src = bank[(i, h)][:].rearrange("p g r u -> p (g r u)").bitcast(BF16)
+                nc.vector.tensor_tensor(out=dst[:, gs, :, :], in0=src.rearrange("p (g r j) -> p g r j", g=2, j=4),
+                                        in1=xsc[:, gs, :].unsqueeze(2).to_broadcast([P, 2, P, 4]), op=ALU.mult)
 
         def quant_x(i):
             xq[i] = work.tile([P, G * P], U32, name="xq", align_bytes=64)
@@ -247,9 +244,9 @@ def tile_mla_pa_w4_kernel(tc, x_bytes, x_scale, wd_words, wd_scales, wk_words, w
                 turn_c(s - 2)
                 copy_ct(s - 2)
             if s < N:
-                product(s)
+                widen(s)
                 turn_x(s)
-                copy_x(s)
+                product(s)
             if 0 <= s - 1 < N:
                 quant_x(s - 1)
                 down(s - 1)

import math
from contextlib import ExitStack

import concourse.mybir as mybir
from concourse.masks import make_identity

F32 = mybir.dt.float32
BF16 = mybir.dt.bfloat16
I32 = mybir.dt.int32
U32 = mybir.dt.uint32
U8 = mybir.dt.uint8
FP8 = mybir.dt.float8_e4m3fn
FP8X4 = mybir.dt.float8_e4m3fn_x4
FP4X4 = mybir.dt.float4_e2m1fn_x4
ALU = mybir.AluOpType
ACT = mybir.ActivationFunctionType

B, S, E, H, DH, L = 2, 512, 2048, 16, 128, 512
NOPE = DH // 4
ROPE = DH - NOPE
HALF = ROPE // 2
THETA = 10000.0
P = 128
T = 2
Q = S // (T * P)
NU = B * Q
G = E // 512
HB = 512 // DH
NG = H // HB

FLOPS = 2 * B * S * E * L + 2 * 2 * B * S * L * H * DH


def tile_mla_pa_w4_kernel(tc, x_bytes, x_scale, wd_words, wd_scales, wk_words, wk_scales,
                                      wv_words, wv_scales, out_k, out_v):
    nc = tc.nc
    with ExitStack() as ctx:
        keep = ctx.enter_context(tc.tile_pool(name="keep", bufs=1))
        xbp = ctx.enter_context(tc.tile_pool(name="xbp", bufs=8))
        work = ctx.enter_context(tc.tile_pool(name="work", bufs=3))
        outp = ctx.enter_context(tc.tile_pool(name="outp", bufs=8))
        ps_x = ctx.enter_context(tc.psum_pool(name="ps_x", bufs=2))
        ps_c = ctx.enter_context(tc.psum_pool(name="ps_c", bufs=2))
        ps_u = ctx.enter_context(tc.psum_pool(name="ps_u", bufs=4))

        ident = keep.tile([P, P], F32, name="ident")
        wd = keep.tile([P, G, 2 * L], U8, name="wd", align_bytes=64)
        wds = keep.tile([P, G, L], U8, name="wds", align_bytes=64)
        wk = keep.tile([P, 2 * H * DH], U8, name="wk", align_bytes=64)
        wks = keep.tile([P, H * DH], U8, name="wks", align_bytes=64)
        wv = keep.tile([P, 2 * H * DH], U8, name="wv", align_bytes=64)
        wvs = keep.tile([P, H * DH], U8, name="wvs", align_bytes=64)
        xsc = keep.tile([P, G, 4], F32, name="xsc")
        xb = [xbp.tile([P, E], U8, name="xb", align_bytes=64) for i in range(NU * T)]

        pos = keep.tile([P, Q, T], F32, name="pos")
        nc.gpsimd.iota(pos[:], pattern=[[T * P, Q], [1, T]], base=0, channel_multiplier=T, allow_small_or_imprecise_dtypes=True)
        nc.gpsimd.memset(wds[:].rearrange("p g n -> p (g n)").bitcast(I32), 0)
        make_identity(nc, ident[:])
        nc.gpsimd.memset(wvs[:].bitcast(I32), 0)
        nc.gpsimd.memset(wks[:].bitcast(I32), 0)

        def load_x(i):
            u, t = divmod(i, T)
            b, q = divmod(u, Q)
            nc.sync.dma_start(out=xb[i][:], in_=x_bytes[b].rearrange("(q p t) k -> q t p k", q=Q, t=T)[q, t])

        load_x(0)
        nc.sync.dma_start(out=xsc[:], in_=x_scale.rearrange("a b (g p t) -> p (a b g) t", p=P, t=4))
        load_x(1)
        nc.sync.dma_start(out=wd[:], in_=wd_words.rearrange("g p n -> p g n"))
        for q in range(4):
            nc.sync.dma_start(out=wds[32 * q:32 * q + 4, :, :].bitcast(I32),
                              in_=wd_scales[:, 4 * q:4 * q + 4, :].rearrange("g q n -> q g n").bitcast(I32))
        load_x(2)
        load_x(3)
        nc.sync.dma_start(out=wv[:], in_=wv_words[0])
        for q in range(4):
            nc.sync.dma_start(out=wvs[32 * q:32 * q + 4, :].bitcast(I32),
                              in_=wv_scales[0, 4 * q:4 * q + 4, :].bitcast(I32))
        nc.sync.dma_start(out=wk[:], in_=wk_words[0])
        for q in range(4):
            nc.sync.dma_start(out=wks[32 * q:32 * q + 4, :].bitcast(I32),
                              in_=wk_scales[0, 4 * q:4 * q + 4, :].bitcast(I32))
        for i in range(4, NU * T):
            load_x(i)

        turn = keep.tile([P, HALF], F32, name="turn")
        ph = keep.tile([P, 2, Q * T, HALF], F32, name="ph")
        phi = keep.tile([P, 2, Q * T, HALF], I32, name="phi")
        over = keep.tile([P, 2, Q * T, HALF], F32, name="over")
        cos = keep.tile([P, Q * T, ROPE], F32, name="cos")
        sin = keep.tile([P, Q * T, ROPE], F32, name="sin")
        warm = keep.tile([P, 1], F32, name="warm")
        nc.vector.memset(warm[:], 0.0)
        nc.scalar.activation(out=warm[:], in_=warm[:], func=ACT.Sin)
        nc.vector.memset(turn[:, 0:1], 1.0)
        n = 1
        while n < HALF:
            m = min(n, HALF - n)
            nc.vector.tensor_scalar(out=turn[:, n:n + m], in0=turn[:, 0:m], scalar1=THETA ** (-2.0 * n / ROPE),
                                    scalar2=None, op0=ALU.mult)
            n += m
        nc.vector.tensor_scalar(out=turn[:], in0=turn[:], scalar1=1.0 / (2.0 * math.pi), scalar2=None, op0=ALU.mult)
        nc.vector.tensor_tensor(out=ph[:, 1, :, :], in0=turn[:].unsqueeze(1).to_broadcast([P, Q * T, HALF]),
                                in1=pos[:].rearrange("p q t -> p (q t)").unsqueeze(2).to_broadcast([P, Q * T, HALF]),
                                op=ALU.mult)
        nc.vector.tensor_scalar(out=ph[:, 0, :, :], in0=ph[:, 1, :, :], scalar1=0.25, scalar2=None, op0=ALU.add)
        nc.vector.tensor_copy(out=phi[:], in_=ph[:])
        nc.vector.tensor_tensor(out=ph[:], in0=ph[:], in1=phi[:], op=ALU.subtract)
        nc.vector.tensor_scalar(out=over[:], in0=ph[:], scalar1=0.5, scalar2=None, op0=ALU.is_gt)
        nc.vector.tensor_tensor(out=ph[:], in0=ph[:], in1=over[:], op=ALU.subtract)
        lo, hi = slice(0, HALF), slice(HALF, ROPE)
        nc.scalar.activation(out=cos[:, :, lo], in_=ph[:, 0, :, :], func=ACT.Sin, scale=2.0 * math.pi)
        nc.scalar.activation(out=cos[:, :, hi], in_=ph[:, 0, :, :], func=ACT.Sin, scale=2.0 * math.pi)
        nc.scalar.activation(out=sin[:, :, lo], in_=ph[:, 1, :, :], func=ACT.Sin, scale=-2.0 * math.pi)
        nc.scalar.activation(out=sin[:, :, hi], in_=ph[:, 1, :, :], func=ACT.Sin, scale=2.0 * math.pi)

        N = NU * T
        xs, xt, xq, xqs, cs, ct, cq, cqs = ({}, {}, {}, {}, {}, {}, {}, {})
        bank, cbank = ({}, {})
        for i in range(N):
            cq[i] = keep.tile([P, P], U32, name="cq%d" % i, align_bytes=64)
            cqs[i] = keep.tile([P, P], U8, name="cqs%d" % i, align_bytes=64)

        def widen(i):
            xs[i] = work.tile([P, E], BF16, name="xs", align_bytes=64)
            if i == 0:
                nc.vector.tensor_copy(out=xs[i][:], in_=xb[i][:].bitcast(FP8))
            else:
                nc.scalar.copy(out=xs[i][:], in_=xb[i][:].bitcast(FP8))

        def turn_x(i):
            words = xs[i][:].bitcast(F32)
            xt[i] = work.tile([P, G * P * 4], BF16, name="xt", align_bytes=64)
            for h in range(2):
                bk = ps_x.tile([P, 2, P, 2], F32, name="xbank")
                for gg in range(2):
                    for u in range(2):
                        g = 2 * h + gg
                        nc.tensor.transpose(bk[:, gg, :, u], words[:, 256 * g + u:256 * (g + 1):2], ident[:])
                bank[(i, h)] = bk

        def product(i):
            dst = xt[i][:].rearrange("p (g r j) -> p g r j", g=G, j=4)
            for h in range(2):
                gs = slice(2 * h, 2 * h + 2)
                src = bank[(i, h)][:].rearrange("p g r u -> p (g r u)").bitcast(BF16)
                nc.vector.tensor_tensor(out=dst[:, gs, :, :], in0=src.rearrange("p (g r j) -> p g r j", g=2, j=4),
                                        in1=xsc[:, gs, :].unsqueeze(2).to_broadcast([P, 2, P, 4]), op=ALU.mult)

        def quant_x(i):
            xq[i] = work.tile([P, G * P], U32, name="xq", align_bytes=64)
            xqs[i] = work.tile([P, G * P], U8, name="xqs", align_bytes=64)
            nc.vector.quantize_mx(out=xq[i][:].bitcast(FP8X4), scales=xqs[i][:], in_=xt[i][:])

        def down(i):
            acc = ps_c.tile([P, L], F32, name="cbank")
            for g in range(G):
                nc.tensor.matmul_mx(out=acc[:], lhsT=xq[i][:, g * P:(g + 1) * P].bitcast(FP8X4),
                                    lhsT_scale=xqs[i][:, g * P:(g + 1) * P],
                                    rhs=wd[:, g, :].bitcast(FP4X4), rhs_scale=wds[:, g, :],
                                    start=(g == 0), stop=(g == G - 1))
            cs[i] = work.tile([P, L], BF16, name="cs", align_bytes=64)
            cbank[i] = acc

        def copy_c(i):
            nc.scalar.copy(out=cs[i][:], in_=cbank[i][:])

        def turn_c(i):
            words = cs[i][:].bitcast(F32)
            bk = ps_c.tile([P, 2, P], F32, name="cbank")
            for u in range(2):
                nc.tensor.transpose(bk[:, u, :], words[:, u:256:2], ident[:])
            cbank[i] = bk

        def copy_ct(i):
            ct[i] = work.tile([P, 4 * P], BF16, name="ct", align_bytes=64)
            nc.scalar.copy(out=ct[i][:].bitcast(F32).rearrange("p (r u) -> p r u", u=2),
                           in_=cbank[i][:].rearrange("p u r -> p r u"))

        def quant_c(i):
            nc.vector.quantize_mx(out=cq[i][:].bitcast(FP8X4), scales=cqs[i][:], in_=ct[i][:])

        okt, ovt = ({}, {})

        def up(i, w, ws, g):
            bk = ps_u.tile([P, 512], F32, name="ubank")
            nc.tensor.matmul_mx(out=bk[:], lhsT=cq[i][:].bitcast(FP8X4), lhsT_scale=cqs[i][:],
                                rhs=w[:, 1024 * g:1024 * (g + 1)].bitcast(FP4X4), rhs_scale=ws[:, 512 * g:512 * (g + 1)],
                                start=True, stop=True)
            return bk

        def store(out, tl, u, g, t0, t1):
            b, q = divmod(u, Q)
            nc.sync.dma_start(
                out=out[b, g * HB:(g + 1) * HB].rearrange("h (q p t) d -> q p h t d", q=Q, t=T)[q, :, :, t0:t1, :]
                .rearrange("p h t d -> p h (t d)"),
                in_=tl[:, :, t0:t1, :].rearrange("p h t d -> p h (t d)"))

        done = {}

        def finish(kind, out, tiles, u, g, t):
            key = (kind, u, g)
            done[key] = done.get(key, 0) + 1
            if done[key] == T:
                store(out, tiles[(u, g)], u, g, 0, T)

        def value(u, g, t):
            bk = up(u * T + t, wv, wvs, g)
            if (u, g) not in ovt:
                ovt[(u, g)] = outp.tile([P, HB, T, DH], F32, name="ov")
            nc.scalar.copy(out=ovt[(u, g)][:, :, t, :], in_=bk[:].rearrange("p (h d) -> p h d", h=HB))
            finish("v", out_v, ovt, u, g, t)

        def key(u, g, t):
            bk = up(u * T + t, wk, wks, g)
            if (u, g) not in okt:
                okt[(u, g)] = outp.tile([P, HB, T, DH], F32, name="ok")
            dst = okt[(u, g)][:, :, t, :]
            src = bk[:].rearrange("p (h d) -> p h d", h=HB)
            rot = src[:, :, NOPE:DH].rearrange("p h (j e) -> p h e j", e=2)
            nc.scalar.copy(out=dst[:, :, 0:NOPE], in_=src[:, :, 0:NOPE])
            w = (u % Q) * T + t
            cosb = cos[:, w, :].rearrange("p (e j) -> p e j", e=2).unsqueeze(1).to_broadcast([P, HB, 2, HALF])
            sinb = sin[:, w, :].rearrange("p (e j) -> p e j", e=2).unsqueeze(1).to_broadcast([P, HB, 2, HALF])
            r1 = work.tile([P, HB, ROPE], F32, name="r1")
            r2 = work.tile([P, HB, ROPE], F32, name="r2")
            nc.vector.tensor_tensor(out=r1[:].rearrange("p h (e j) -> p h e j", e=2), in0=rot, in1=cosb, op=ALU.mult)
            nc.vector.tensor_tensor(out=r2[:].rearrange("p h (e j) -> p h e j", e=2), in0=rot[:, :, ::-1, :], in1=sinb,
                                    op=ALU.mult)
            last = (u, g, t) == (NU - 1, NG - 1, T - 1)
            adder = nc.vector if last else nc.gpsimd
            adder.tensor_tensor(out=dst[:, :, NOPE:DH], in0=r1[:], in1=r2[:], op=ALU.add)
            finish("k", out_k, okt, u, g, t)

        order = [(0, 0), (1, 0), (0, 1), (1, 1), (2, 0), (3, 0), (2, 1), (3, 1)]
        keys = [(u, g, t) for u in range(NU) for g, t in order]
        vals = [(u, g, t) for u in range(NU) for g, t in order]
        n_keys = [0, 0, 0, 2, 4, 4, 4, 4]
        n_vals = [0, 0, 0, 2, 4, 4, 4, 4]
        for s in range(N + 3):
            if 0 <= s - 2 < N:
                turn_c(s - 2)
                copy_ct(s - 2)
            if s < N:
                widen(s)
                turn_x(s)
                product(s)
            if 0 <= s - 1 < N:
                quant_x(s - 1)
                down(s - 1)
                copy_c(s - 1)
            nk = n_keys[s] if s < N else 2
            nv = n_vals[s] if s < N else 2
            for r in range(max(nk, nv)):
                if r < nv:
                    value(*vals.pop(0))
                if r < nk:
                    key(*keys.pop(0))
            if 0 <= s - 2 < N:
                quant_c(s - 2)
        while keys or vals:
            if vals:
                value(*vals.pop(0))
            if keys:
                key(*keys.pop(0))
